import numpy as np
import ml_dtypes


def mxq(x, axis, fmt="e4m3"):
    dtype, down = {"e4m3": (ml_dtypes.float8_e4m3fn, 7), "e5m2": (ml_dtypes.float8_e5m2, 14)}[fmt]
    v = np.moveaxis(np.asarray(x, np.float32).astype(ml_dtypes.bfloat16).astype(np.float64), axis, -1)
    blocks = v.reshape(v.shape[:-1] + (-1, 32))
    amax = np.abs(blocks).max(-1, keepdims=True)
    byte = np.maximum(np.where(amax > 0, np.frexp(amax)[1] - 1 + 127, 0) - down, 1)
    scale = np.exp2(byte - 127.0)
    codes = (blocks / scale).astype(np.float32).astype(dtype).astype(np.float64)
    return np.moveaxis((codes * scale).reshape(v.shape), -1, axis)


WIDE = False


def mx_kscale(k):
    if not WIDE:
        return np.ones(k)
    levels = np.array([10, -10, 5, -5, 0])
    if k % 512:
        return np.exp2(np.random.permutation(np.resize(levels, k // 32))).repeat(32)
    a = np.empty((k // 512, 16))
    for p in range(k // 512):
        a[p, :8] = np.random.permutation(np.resize(levels, 8))
        for g in range(8):
            far = levels[np.abs(levels - a[p, g]) >= 10]
            a[p, g + 8] = far[np.random.randint(len(far))]
    return np.exp2(a.ravel()).repeat(32)


BF16 = ml_dtypes.bfloat16


def bf(x):
    return np.asarray(x, np.float32).astype(BF16)


def f64(x):
    return np.asarray(x).astype(np.float64)


I, H, B = 2048, 2048, 128


def sigmoid(v):
    return 1.0 / (1.0 + np.exp(-v))


def setup_inputs():
    s, t = mx_kscale(I), mx_kscale(H)
    d = {"x": bf(np.random.standard_normal((I, B)) * s[:, None]), "h": bf(np.random.standard_normal((B, H)) * t[None, :]),
         "c": bf(np.random.standard_normal((B, H))), "ig": bf(np.random.standard_normal((H, B)) * 0.35)}
    for n in ("w_if", "w_io"):
        d[n] = bf(np.random.standard_normal((H, I)) * 0.7 / np.sqrt(I) / s[None, :])
    for n in ("w_hf", "w_ho"):
        d[n] = bf(np.random.standard_normal((H, H)) * 0.7 / np.sqrt(H) / t[None, :])
    for n in ("b_if", "b_hf", "b_io", "b_ho"):
        d[n] = bf(np.random.standard_normal((H, 1)) * 0.3)
    return d


def reference(x, h, c, ig, w_if, w_io, w_hf, w_ho, b_if, b_hf, b_io, b_ho):
    xq = mxq(f64(x), 0, "e4m3")
    hq = mxq(f64(h).T, 0, "e4m3")
    f = sigmoid((mxq(f64(w_if), 1, "e4m3") @ xq) + f64(b_if) + (mxq(f64(w_hf), 1, "e4m3") @ hq) + f64(b_hf))
    o = sigmoid((mxq(f64(w_io), 1, "e4m3") @ xq) + f64(b_io) + (mxq(f64(w_ho), 1, "e4m3") @ hq) + f64(b_ho))
    c_next_t = f * f64(c).T + f64(ig)
    h_next_t = o * np.tanh(c_next_t)
    return h_next_t.T, c_next_t.T

@@ -1,0 +1,442 @@
+from contextlib import ExitStack
+
+import concourse.mybir as mybir
+from concourse.masks import make_identity
+
+F32 = mybir.dt.float32
+BF16 = mybir.dt.bfloat16
+U32 = mybir.dt.uint32
+U8 = mybir.dt.uint8
+I32 = mybir.dt.int32
+FP8X4 = mybir.dt.float8_e4m3fn_x4
+ACT = mybir.ActivationFunctionType
+ALU = mybir.AluOpType
+
+P = 128
+K = 2048
+HID = 2048
+NCOL = 512
+WBUFS = 6
+V_BANKS = (1, 5)
+V_BANKS_EARLY = (1, 5)
+EARLY_UNITS = 6
+SPLIT_CHUNKS = ()
+BIAS_AT = (2, 2, 3, 3, 4, 4, 5, 5)
+X_AT = 1
+H_AT = 2
+IG_AT = 4
+
+FLOPS = 2 * 4 * 2048 * 2048 * 128
+
+CHUNKS = (
+    (0, 0), (1, 0), (2, 0), (3, 0),
+    (0, 1), (1, 1), (2, 1), (3, 1),
+    (0, 2), (1, 2), (0, 3), (1, 3),
+    (2, 2), (3, 2), (2, 3), (3, 3),
+)
+ACC_BANK = {(0, 0): 0, (1, 0): 1, (0, 1): 0, (1, 1): 1, (0, 2): 0, (0, 3): 1, (1, 2): 0, (1, 3): 1}
+LAST = len(CHUNKS) - 1
+
+
+def tile_naivelstm_pb_kernel(
+    tc, x, h, c, ig, w_if, w_io, w_hf, w_ho, b_if, b_hf, b_io, b_ho, out_0, out_1
+):
+    nc = tc.nc
+    with ExitStack() as ctx:
+        ctx.enter_context(tc.manual_schedule())
+        const = ctx.enter_context(tc.tile_pool(name="const", bufs=1))
+        wpool = ctx.enter_context(tc.tile_pool(name="wpool", bufs=WBUFS))
+        gpool = ctx.enter_context(tc.tile_pool(name="gpool", bufs=3))
+        cpool = ctx.enter_context(tc.tile_pool(name="cpool", bufs=6))
+        ep = ctx.enter_context(tc.tile_pool(name="ep", bufs=2))
+        accp = ctx.enter_context(tc.psum_pool(name="accp", bufs=1))
+        tp = ctx.enter_context(tc.psum_pool(name="tp", bufs=6))
+
+        weights = (w_if, w_hf, w_io, w_ho)
+
+        ident32 = const.tile([P, P], F32, name="ident32")
+        identb = const.tile([P, P], BF16, name="identb")
+        brows = const.tile([P, NCOL], BF16, name="brows")
+        nc.vector.memset(brows[:].bitcast(I32), 0)
+        for first_row, b in ((0, b_if), (1, b_hf), (2, b_io), (3, b_ho)):
+            nc.scalar.dma_start(
+                out=brows[first_row : 16 : 4, :], in_=b.rearrange("(a n) o -> a (n o)", a=4)
+            )
+        make_identity(nc, identb[:])
+        make_identity(nc, ident32[:])
+        pairsel = const.tile([P, 8], BF16, name="pairsel")
+        nc.vector.tensor_tensor(out=pairsel[:], in0=identb[:, 0:16:2], in1=identb[:, 1:16:2], op=ALU.add)
+        warm = const.tile([P, 2], F32, name="warm")
+        nc.vector.memset(warm[:], 0.0)
+        nc.scalar.activation(out=warm[:, 1:2], in_=warm[:, 0:1], func=ACT.Sigmoid)
+
+        loads = []
+        units = []
+        for ci in range(LAST):
+            if ci in SPLIT_CHUNKS:
+                for gp in range(2):
+                    units.append((len(loads), "half", ci, gp))
+                    loads.append(("half", ci, gp))
+            else:
+                for gp in range(2):
+                    units.append((len(loads), "whole", ci, gp))
+                loads.append(("whole", ci, 0))
+        NMAIN = len(units)
+        for j in range(4):
+            units.append((len(loads), "block", LAST, j))
+            loads.append(("block", LAST, j))
+        last_unit_of_load = {}
+        for k in range(len(units)):
+            last_unit_of_load[units[k][0]] = k
+
+        wt = {}
+        stores = {"open": False, "pending": []}
+
+        def load(n):
+            kind, ci, part = loads[n]
+            wsel, a = CHUNKS[ci]
+            w = weights[wsel]
+            if kind == "whole":
+                t = wpool.tile([P, 4 * K], BF16, name="wt", tag="wt")
+                nc.sync.dma_start(
+                    out=t[:], in_=w.rearrange("(a q j) k -> a q (j k)", a=4, q=P, j=4)[a, :, :]
+                )
+            elif kind == "half":
+                t = wpool.tile([P, 4, K // 2], BF16, name="wt", tag="wt")
+                nc.sync.dma_start(
+                    out=t[:],
+                    in_=w.rearrange("(a q j) k -> a q j k", a=4, q=P, j=4)[
+                        a, :, :, part * (K // 2) : (part + 1) * (K // 2)
+                    ],
+                )
+            else:
+                t = wpool.tile([P, K], BF16, name="wt", tag="wt")
+                nc.sync.dma_start(out=t[:], in_=w[a * NCOL + part * P : a * NCOL + (part + 1) * P, :])
+            wt[n] = t
+            if n == len(loads) - 1:
+                stores["open"] = True
+                for dst, src in stores["pending"]:
+                    nc.sync.dma_start(out=dst, in_=src)
+
+        def store(dst, src):
+            if stores["open"]:
+                nc.sync.dma_start(out=dst, in_=src)
+            else:
+                stores["pending"].append((dst, src))
+
+        h_sb = const.tile([P, K], BF16, name="h_sb")
+        xraw = const.tile([P, 4, 4, P], BF16, name="xraw")
+        ig_sb = const.tile([P, 4, 4 * P], BF16, name="ig_sb")
+        c_sb = const.tile([P, HID], BF16, name="c_sb")
+        load(0)
+        nc.sync.dma_start(out=xraw[:], in_=x.rearrange("(g p t) b -> p g t b", g=4, p=P, t=4))
+        load(1)
+        nc.sync.dma_start(out=h_sb[:], in_=h)
+        load(2)
+        nc.sync.dma_start(out=ig_sb[:], in_=ig.rearrange("(a q j) b -> q a (j b)", a=4, q=P, j=4))
+        nc.sync.dma_start(out=c_sb[:], in_=c)
+        load(3)
+        load(4)
+        progress = {"loaded": 5, "freed": 0}
+
+        def loads_after(k):
+            if last_unit_of_load[units[k][0]] == k:
+                progress["freed"] = progress["freed"] + 1
+            while progress["loaded"] < len(loads) and progress["loaded"] - progress["freed"] < WBUFS:
+                load(progress["loaded"])
+                progress["loaded"] = progress["loaded"] + 1
+
+        while progress["loaded"] < WBUFS:
+            load(progress["loaded"])
+            progress["loaded"] = progress["loaded"] + 1
+
+        def transpose_bank(src32, cols):
+            bank = tp.tile([P, 2, 2, P], F32, name="xt", tag="xt")
+            for u in range(2):
+                for s in range(2):
+                    col = cols[u][s]
+                    nc.tensor.transpose(bank[:, u, s, :], src32[:, col : col + 2 * P - 1 : 2], ident32[:])
+            return bank
+
+        def copy_bank(eng, grouped, slot, bank):
+            dst = grouped[:].bitcast(F32).rearrange("p (n u) -> p n u", u=2)
+            dst = dst[:, slot * 256 : (slot + 1) * 256, :]
+            src = bank[:].rearrange("p u s q -> p (s q) u")
+            if eng == "S":
+                nc.scalar.copy(out=dst, in_=src)
+            else:
+                nc.vector.tensor_copy(out=dst, in_=src)
+
+        def row_block_cols(gp):
+            return [[(2 * gp + s) * 2 * P + u for s in range(2)] for u in range(2)]
+
+        act_codes = []
+        act_scales = []
+        for nm in ("x", "h"):
+            act_codes.append(const.tile([P, 512], U32, name="codes_" + nm, align_bytes=64))
+            act_scales.append(const.tile([P, 512], U8, name="scales_" + nm, align_bytes=64))
+        act_grouped = {}
+
+        def prepare_x():
+            xg = gpool.tile([P, K], BF16, name="grouped", tag="grouped", align_bytes=64)
+            nc.vector.tensor_copy(
+                out=xg[:].rearrange("p (g b t) -> p g b t", g=4, b=P, t=4),
+                in_=xraw[:].rearrange("p g t b -> p g b t"),
+            )
+            act_grouped[0] = xg
+
+        def prepare_h():
+            h32 = h_sb[:].bitcast(F32)
+            hg = gpool.tile([P, K], BF16, name="grouped", tag="grouped", align_bytes=64)
+            hbanks = [transpose_bank(h32, row_block_cols(gp)) for gp in range(2)]
+            for gp in range(2):
+                copy_bank("SV"[gp], hg, gp, hbanks[gp])
+            act_grouped[1] = hg
+
+        def quantise_act(opnd):
+            nc.vector.quantize_mx(
+                out=act_codes[opnd][:].bitcast(FP8X4), scales=act_scales[opnd][:], in_=act_grouped[opnd][:]
+            )
+
+        igT = const.tile([P, 4, 4, P], BF16, name="igT")
+
+        def prepare_ig():
+            for half in range(2):
+                ibank = tp.tile([P, 2, 4, P], BF16, name="ibank", tag="xt")
+                for a2 in range(2):
+                    for j in range(4):
+                        nc.tensor.transpose(
+                            ibank[:, a2, j, :],
+                            ig_sb[:, 2 * half + a2, j * P : (j + 1) * P],
+                            identb[:],
+                        )
+                nc.scalar.copy(out=igT[:, 2 * half : 2 * half + 2, :, :], in_=ibank[:])
+
+        bias = const.tile([P, 2 * HID], F32, name="bias")
+
+        def spread_bias(gate, a):
+            cols = slice(gate * HID + a * NCOL, gate * HID + (a + 1) * NCOL)
+            bbank = tp.tile([P, NCOL], F32, name="bbank", tag="xt")
+            i = 2 * a + gate
+            nc.tensor.matmul(
+                out=bbank[:], lhsT=pairsel[:, i : i + 1].to_broadcast([P, P]), rhs=brows[:], start=True, stop=True
+            )
+            nc.scalar.copy(out=bias[:, cols], in_=bbank[:])
+
+        cn_all = const.tile([P, HID], F32, name="cn_all")
+        hn_all = const.tile([P, HID], F32, name="hn_all")
+        grouped = {}
+        codes = {}
+        scales = {}
+        acc = {}
+        state = {}
+        th = {}
+        blk = {}
+        deferred = {}
+        banks_done = {"n": 0}
+
+        def defer(slot, fn):
+            deferred[slot] = deferred.get(slot, []) + [fn]
+
+        def late(slot):
+            for fn in deferred.get(slot, []):
+                fn()
+
+        def unit_t(k, engines=None):
+            n, kind, ci, part = units[k]
+            w32 = wt[n][:]
+            if kind == "half":
+                w32 = w32.rearrange("p j k -> p (j k)")
+            w32 = w32.bitcast(F32)
+            if kind == "block":
+                grouped[k] = gpool.tile([P, K], BF16, name="grouped", tag="grouped", align_bytes=64)
+                colmaps = [row_block_cols(gp) for gp in range(2)]
+            else:
+                grouped[k] = gpool.tile([P, 2 * K], BF16, name="grouped", tag="grouped", align_bytes=64)
+                rowlen = 1024 if kind == "whole" else 512
+                first = 2 * part if kind == "whole" else 0
+                colmaps = [
+                    [[(2 * jp + s) * rowlen + (first + gg) * 2 * P + u for s in range(2)] for u in range(2)]
+                    for gg in range(2)
+                    for jp in range(2)
+                ]
+            for slot in range(len(colmaps)):
+                bank = transpose_bank(w32, colmaps[slot])
+                if engines is None and k >= NMAIN - 1:
+                    eng = "S"
+                elif engines is None:
+                    eng = "V" if banks_done["n"] % 8 in (V_BANKS_EARLY if k < EARLY_UNITS else V_BANKS) else "S"
+                else:
+                    eng = engines[slot]
+                banks_done["n"] = banks_done["n"] + 1
+                copy_bank(eng, grouped[k], slot, bank)
+
+        def unit_q(k):
+            width = NCOL if units[k][1] == "block" else 2 * NCOL
+            codes[k] = cpool.tile([P, width], U32, name="codes", tag="codes", align_bytes=64)
+            scales[k] = cpool.tile([P, width], U8, name="scales", tag="scales", align_bytes=64)
+            nc.vector.quantize_mx(
+                out=codes[k][:].bitcast(FP8X4), scales=scales[k][:], in_=grouped[k][:]
+            )
+
+        def mx(out, opnd, g, k, cols, start, stop):
+            nc.tensor.matmul_mx(
+                out=out,
+                lhsT=act_codes[opnd][:, g * P : (g + 1) * P].bitcast(FP8X4),
+                lhsT_scale=act_scales[opnd][:, g * P : (g + 1) * P],
+                rhs=codes[k][:, cols].bitcast(FP8X4),
+                rhs_scale=scales[k][:, cols],
+                start=start,
+                stop=stop,
+            )
+
+        def chunk_mx(ci):
+            wsel, a = CHUNKS[ci]
+            gate, opnd = divmod(wsel, 2)
+            alone = (wsel, a) == (2, 3)
+            if opnd == 0:
+                bank = ACC_BANK[(gate, a)]
+                acc[gate] = accp.tile([P, NCOL], F32, name="acc%d" % bank, tag="acc%d" % bank)
+            for g in range(4):
+                mx(
+                    acc[gate][:], opnd, g, 2 * ci + g // 2, slice((g % 2) * NCOL, (g % 2 + 1) * NCOL),
+                    opnd == 0 and g == 0, (opnd == 1 or alone) and g == 3,
+                )
+
+        def block_mx(j):
+            if j == 0:
+                blk[j] = accp.tile([P, P], F32, name="acc0", tag="acc0")
+            else:
+                blk[j] = tp.tile([P, P], F32, name="blk", tag="xt")
+            for g in range(4):
+                mx(blk[j][:], 1, g, NMAIN + j, slice(g * P, (g + 1) * P), g == 0, g == 3)
+
+        def natural(ap):
+            return ap.rearrange("p (q j) -> p q j", j=4)
+
+        def ep_z(a, gate):
+            z = ep.tile([P, NCOL], F32, name="z", tag="z")
+            nc.vector.tensor_tensor(
+                out=natural(z[:]),
+                in0=acc[gate][:].rearrange("p (j q) -> p q j", j=4),
+                in1=natural(bias[:, gate * HID + a * NCOL : gate * HID + (a + 1) * NCOL]),
+                op=ALU.add,
+            )
+            state["z"] = z
+
+        def ep_sig():
+            s = ep.tile([P, NCOL], F32, name="sg", tag="sg")
+            nc.scalar.activation(out=s[:], in_=state["z"][:], func=ACT.Sigmoid)
+            state["s"] = s
+
+        def ep_cnext(a):
+            cols = slice(a * NCOL, (a + 1) * NCOL)
+            t = ep.tile([P, NCOL], F32, name="fc", tag="fc")
+            nc.vector.tensor_tensor(out=t[:], in0=state["s"][:], in1=c_sb[:, cols], op=ALU.mult)
+            nc.vector.tensor_tensor(
+                out=natural(cn_all[:, cols]),
+                in0=natural(t[:]),
+                in1=igT[:, a, :, :].rearrange("p j q -> p q j"),
+                op=ALU.add,
+            )
+
+        def ep_tanh(a):
+            cols = slice(a * NCOL, (a + 1) * NCOL)
+            if a == 3:
+                store(out_1, cn_all[:])
+            th[a] = ep.tile([P, NCOL], F32, name="th", tag="th")
+            nc.scalar.activation(out=th[a][:], in_=cn_all[:, cols], func=ACT.Tanh)
+
+        def ep_hnext(a):
+            cols = slice(a * NCOL, (a + 1) * NCOL)
+            nc.vector.tensor_tensor(out=hn_all[:, cols], in0=state["s"][:], in1=th[a][:], op=ALU.mult)
+            if a == 2:
+                store(out_0[:, 0 : 3 * NCOL], hn_all[:, 0 : 3 * NCOL])
+
+        def schedule_epilogue(slot, ci):
+            wsel, a = CHUNKS[ci]
+            if wsel == 1:
+                defer(slot + 1, lambda: ep_z(a, 0))
+                defer(slot + 2, ep_sig)
+                defer(slot + 3, lambda: ep_cnext(a))
+                defer(slot + 4, lambda: ep_tanh(a))
+            if wsel == 3:
+                defer(slot + 1, lambda: ep_z(a, 1))
+                defer(slot + 2, ep_sig)
+                defer(slot + 3, lambda: ep_hnext(a))
+
+        def last_z(j):
+            zl = ep.tile([P, P], F32, name="zl", tag="zl", bufs=4)
+            nc.vector.tensor_tensor(
+                out=zl[:], in0=blk[j][:], in1=state["zpart"][:, j * P : (j + 1) * P], op=ALU.add
+            )
+            state["zl%d" % j] = zl
+
+        def last_sig(j):
+            sl = ep.tile([P, P], F32, name="sl", tag="sl", bufs=4)
+            nc.scalar.activation(out=sl[:], in_=state["zl%d" % j][:], func=ACT.Sigmoid)
+            state["sl%d" % j] = sl
+
+        def last_h(j):
+            cols = slice(3 * NCOL + j * P, 3 * NCOL + (j + 1) * P)
+            nc.vector.tensor_tensor(
+                out=hn_all[:, cols], in0=state["sl%d" % j][:], in1=th[3][:, j * P : (j + 1) * P], op=ALU.mult
+            )
+            if j == 2:
+                store(out_0[:, 3 * NCOL : 3 * NCOL + 3 * P], hn_all[:, 3 * NCOL : 3 * NCOL + 3 * P])
+            if j == 3:
+                store(out_0[:, cols], hn_all[:, cols])
+
+        for k in range(NMAIN):
+            unit_t(k)
+            loads_after(k)
+            if k >= 1:
+                unit_q(k - 1)
+            if k == X_AT:
+                prepare_x()
+            if k == H_AT:
+                prepare_h()
+            if k == X_AT + 1:
+                quantise_act(0)
+            if k == H_AT + 1:
+                quantise_act(1)
+            if k == IG_AT:
+                prepare_ig()
+            for n in range(8):
+                if BIAS_AT[n] == k:
+                    spread_bias(n % 2, n // 2)
+            if k % 2 == 1 and k >= 3:
+                chunk_mx((k - 3) // 2)
+                schedule_epilogue(k, (k - 3) // 2)
+            late(k)
+
+        unit_t(NMAIN, "SS")
+        loads_after(NMAIN)
+        unit_q(NMAIN - 1)
+        late(NMAIN)
+        unit_t(NMAIN + 1, "SS")
+        loads_after(NMAIN + 1)
+        unit_q(NMAIN)
+        chunk_mx(LAST - 1)
+        late(NMAIN + 1)
+        unit_t(NMAIN + 2, "SS")
+        unit_q(NMAIN + 1)
+        late(NMAIN + 2)
+        ep_z(3, 1)
+        state["zpart"] = state["z"]
+        unit_t(NMAIN + 3, "SS")
+        unit_q(NMAIN + 2)
+        late(NMAIN + 3)
+        for j in range(3):
+            block_mx(j)
+        unit_q(NMAIN + 3)
+        block_mx(3)
+        for j in range(3):
+            last_z(j)
+            last_sig(j)
+        last_h(0)
+        last_h(1)
+        last_z(3)
+        last_sig(3)
+        last_h(2)
+        last_h(3)

@@ -17,9 +17,10 @@ K = 2048
 HID = 2048
 NCOL = 512
 WBUFS = 6
-V_BANKS = (1, 5)
+V_BANKS = (1,)
 V_BANKS_EARLY = (1, 5)
 EARLY_UNITS = 6
+REORDER_FROM = 6
 SPLIT_CHUNKS = ()
 BIAS_AT = (2, 2, 3, 3, 4, 4, 5, 5)
 X_AT = 1
@@ -47,7 +48,8 @@ def tile_naivelstm_pb_kernel(
         const = ctx.enter_context(tc.tile_pool(name="const", bufs=1))
         wpool = ctx.enter_context(tc.tile_pool(name="wpool", bufs=WBUFS))
         gpool = ctx.enter_context(tc.tile_pool(name="gpool", bufs=3))
-        cpool = ctx.enter_context(tc.tile_pool(name="cpool", bufs=6))
+        rpool = ctx.enter_context(tc.tile_pool(name="rpool", bufs=3))
+        cpool = ctx.enter_context(tc.tile_pool(name="cpool", bufs=5))
         ep = ctx.enter_context(tc.tile_pool(name="ep", bufs=2))
         accp = ctx.enter_context(tc.psum_pool(name="accp", bufs=1))
         tp = ctx.enter_context(tc.psum_pool(name="tp", bufs=6))
@@ -150,12 +152,12 @@ def tile_naivelstm_pb_kernel(
             load(progress["loaded"])
             progress["loaded"] = progress["loaded"] + 1
 
-        def transpose_bank(src32, cols):
+        def transpose_bank(src32, cols, step=2):
             bank = tp.tile([P, 2, 2, P], F32, name="xt", tag="xt")
             for u in range(2):
                 for s in range(2):
                     col = cols[u][s]
-                    nc.tensor.transpose(bank[:, u, s, :], src32[:, col : col + 2 * P - 1 : 2], ident32[:])
+                    nc.tensor.transpose(bank[:, u, s, :], src32[:, col : col + step * (P - 1) + 1 : step], ident32[:])
             return bank
 
         def copy_bank(eng, grouped, slot, bank):
@@ -242,6 +244,19 @@ def tile_naivelstm_pb_kernel(
             for fn in deferred.get(slot, []):
                 fn()
 
+        ordered = {}
+
+        def is_reordered(k):
+            return k >= REORDER_FROM and k < NMAIN
+
+        def unit_r(k):
+            n, kind, ci, part = units[k]
+            g = 2 * part + 1
+            t = rpool.tile([P, 4, 2, P], F32, name="ordered", tag="ordered")
+            src = wt[n][:].bitcast(F32).rearrange("q (j g p u) -> q g j u p", j=4, g=4, u=2)
+            nc.vector.tensor_copy(out=t[:], in_=src[:, g, :, :, :])
+            ordered[k] = t
+
         def unit_t(k, engines=None):
             n, kind, ci, part = units[k]
             w32 = wt[n][:]
@@ -261,7 +276,13 @@ def tile_naivelstm_pb_kernel(
                     for jp in range(2)
                 ]
             for slot in range(len(colmaps)):
-                bank = transpose_bank(w32, colmaps[slot])
+                if is_reordered(k) and slot >= 2:
+                    jp = slot - 2
+                    flat = ordered[k][:].rearrange("q j u p -> q (j u p)")
+                    cols = [[((2 * jp + s) * 2 + u) * P for s in range(2)] for u in range(2)]
+                    bank = transpose_bank(flat, cols, 1)
+                else:
+                    bank = transpose_bank(w32, colmaps[slot])
                 if engines is None and k >= NMAIN - 1:
                     eng = "S"
                 elif engines is None:
@@ -388,6 +409,8 @@ def tile_naivelstm_pb_kernel(
                 store(out_0[:, cols], hn_all[:, cols])
 
         for k in range(NMAIN):
+            if is_reordered(k + 1):
+                unit_r(k + 1)
             unit_t(k)
             loads_after(k)
             if k >= 1:

@@ -17,25 +17,21 @@ K = 2048
 HID = 2048
 NCOL = 512
 WBUFS = 6
-V_BANKS = (1,)
-V_BANKS_EARLY = (1, 5)
+V_BANKS = (2,)
+V_BANKS_EARLY = (1, 5, 9, 13)
 EARLY_UNITS = 6
 REORDER_FROM = 6
-SPLIT_CHUNKS = ()
-BIAS_AT = (2, 2, 3, 3, 4, 4, 5, 5)
-X_AT = 1
-H_AT = 2
-IG_AT = 4
+PIECES = {
+    0: ((0, 0, 2), (0, 2, 4), (1, 0, 2), (1, 2, 4)),
+    1: ((0, 0, 4), (1, 0, 4)),
+}
+BIAS_AT = (2, 2, 2, 2, 3, 3, 4, 4)
+X_AT = 2
+IG_AT = 7
 
 FLOPS = 2 * 4 * 2048 * 2048 * 128
 
-CHUNKS = (
-    (0, 0), (1, 0), (2, 0), (3, 0),
-    (0, 1), (1, 1), (2, 1), (3, 1),
-    (0, 2), (1, 2), (0, 3), (1, 3),
-    (2, 2), (3, 2), (2, 3), (3, 3),
-)
-ACC_BANK = {(0, 0): 0, (1, 0): 1, (0, 1): 0, (1, 1): 1, (0, 2): 0, (0, 3): 1, (1, 2): 0, (1, 3): 1}
+CHUNKS = [(2 * gate + opnd, a) for gate in range(2) for a in range(4) for opnd in range(2)]
 LAST = len(CHUNKS) - 1
 
 
@@ -72,50 +68,40 @@ def tile_naivelstm_pb_kernel(
         nc.vector.memset(warm[:], 0.0)
         nc.scalar.activation(out=warm[:, 1:2], in_=warm[:, 0:1], func=ACT.Sigmoid)
 
-        loads = []
-        units = []
-        for ci in range(LAST):
-            if ci in SPLIT_CHUNKS:
-                for gp in range(2):
-                    units.append((len(loads), "half", ci, gp))
-                    loads.append(("half", ci, gp))
-            else:
-                for gp in range(2):
-                    units.append((len(loads), "whole", ci, gp))
-                loads.append(("whole", ci, 0))
+        units = [("wide", ci, gp) for ci in range(LAST) for gp in range(2)]
         NMAIN = len(units)
-        for j in range(4):
-            units.append((len(loads), "block", LAST, j))
-            loads.append(("block", LAST, j))
-        last_unit_of_load = {}
-        for k in range(len(units)):
-            last_unit_of_load[units[k][0]] = k
+        units = units + [("block", LAST, j) for j in range(4)]
 
         wt = {}
+        pieces_of = {}
         stores = {"open": False, "pending": []}
 
-        def load(n):
-            kind, ci, part = loads[n]
+        def weight_tile(ci):
+            wt[ci] = wpool.tile([P, 4 * K], BF16, name="wt", tag="wt")
             wsel, a = CHUNKS[ci]
-            w = weights[wsel]
-            if kind == "whole":
-                t = wpool.tile([P, 4 * K], BF16, name="wt", tag="wt")
-                nc.sync.dma_start(
-                    out=t[:], in_=w.rearrange("(a q j) k -> a q (j k)", a=4, q=P, j=4)[a, :, :]
-                )
-            elif kind == "half":
-                t = wpool.tile([P, 4, K // 2], BF16, name="wt", tag="wt")
-                nc.sync.dma_start(
-                    out=t[:],
-                    in_=w.rearrange("(a q j) k -> a q j k", a=4, q=P, j=4)[
-                        a, :, :, part * (K // 2) : (part + 1) * (K // 2)
-                    ],
-                )
+            return wt[ci][:], weights[wsel][a * NCOL : (a + 1) * NCOL, :]
+
+        def load_piece(ci, i):
+            half, j0, j1 = PIECES[ci][i]
+            if i == 0:
+                pieces_of[ci] = weight_tile(ci)
+            t, rows = pieces_of[ci]
+            nc.sync.dma_start(
+                out=t.rearrange("q (h j k) -> q h j k", h=2, j=4)[:, half, j0:j1, :],
+                in_=rows.rearrange("(q j) (h k) -> q h j k", j=4, h=2)[:, half, j0:j1, :],
+            )
+
+        def load(ci):
+            if ci in PIECES:
+                for i in range(len(PIECES[ci])):
+                    load_piece(ci, i)
+                return
+            t, rows = weight_tile(ci)
+            if ci < LAST:
+                nc.sync.dma_start(out=t, in_=rows.rearrange("(q j) k -> q (j k)", j=4))
             else:
-                t = wpool.tile([P, K], BF16, name="wt", tag="wt")
-                nc.sync.dma_start(out=t[:], in_=w[a * NCOL + part * P : a * NCOL + (part + 1) * P, :])
-            wt[n] = t
-            if n == len(loads) - 1:
+                for j in range(4):
+                    nc.sync.dma_start(out=t[:, j * K : (j + 1) * K], in_=rows[j * P : (j + 1) * P, :])
                 stores["open"] = True
                 for dst, src in stores["pending"]:
                     nc.sync.dma_start(out=dst, in_=src)
@@ -130,21 +116,21 @@ def tile_naivelstm_pb_kernel(
         xraw = const.tile([P, 4, 4, P], BF16, name="xraw")
         ig_sb = const.tile([P, 4, 4 * P], BF16, name="ig_sb")
         c_sb = const.tile([P, HID], BF16, name="c_sb")
-        load(0)
-        nc.sync.dma_start(out=xraw[:], in_=x.rearrange("(g p t) b -> p g t b", g=4, p=P, t=4))
-        load(1)
         nc.sync.dma_start(out=h_sb[:], in_=h)
+        load(0)
+        load_piece(1, 0)
+        nc.sync.dma_start(out=xraw[:], in_=x.rearrange("(g p t) b -> p g t b", g=4, p=P, t=4))
+        load_piece(1, 1)
         load(2)
+        load(3)
         nc.sync.dma_start(out=ig_sb[:], in_=ig.rearrange("(a q j) b -> q a (j b)", a=4, q=P, j=4))
         nc.sync.dma_start(out=c_sb[:], in_=c)
-        load(3)
-        load(4)
-        progress = {"loaded": 5, "freed": 0}
+        progress = {"loaded": 4, "freed": 0}
 
         def loads_after(k):
-            if last_unit_of_load[units[k][0]] == k:
+            if k % 2 == 1 and k < NMAIN:
                 progress["freed"] = progress["freed"] + 1
-            while progress["loaded"] < len(loads) and progress["loaded"] - progress["freed"] < WBUFS:
+            while progress["loaded"] <= LAST and progress["loaded"] - progress["freed"] < WBUFS:
                 load(progress["loaded"])
                 progress["loaded"] = progress["loaded"] + 1
 
@@ -192,7 +178,7 @@ def tile_naivelstm_pb_kernel(
             hg = gpool.tile([P, K], BF16, name="grouped", tag="grouped", align_bytes=64)
             hbanks = [transpose_bank(h32, row_block_cols(gp)) for gp in range(2)]
             for gp in range(2):
-                copy_bank("SV"[gp], hg, gp, hbanks[gp])
+                copy_bank("V", hg, gp, hbanks[gp])
             act_grouped[1] = hg
 
         def quantise_act(opnd):
@@ -250,50 +236,65 @@ def tile_naivelstm_pb_kernel(
             return k >= REORDER_FROM and k < NMAIN
 
         def unit_r(k):
-            n, kind, ci, part = units[k]
+            kind, ci, part = units[k]
             g = 2 * part + 1
             t = rpool.tile([P, 4, 2, P], F32, name="ordered", tag="ordered")
-            src = wt[n][:].bitcast(F32).rearrange("q (j g p u) -> q g j u p", j=4, g=4, u=2)
+            src = wt[ci][:].bitcast(F32).rearrange("q (j g p u) -> q g j u p", j=4, g=4, u=2)
             nc.vector.tensor_copy(out=t[:], in_=src[:, g, :, :, :])
             ordered[k] = t
 
+        def word_of(ci, j, g):
+            if ci in PIECES:
+                return (g // 2) * 2048 + j * 512 + (g % 2) * 256
+            return j * 1024 + g * 256
+
+        vector_copies = []
+
+        def late_vector_copies():
+            for dst, slot, bank in vector_copies:
+                copy_bank("V", dst, slot, bank)
+            vector_copies.clear()
+
         def unit_t(k, engines=None):
-            n, kind, ci, part = units[k]
-            w32 = wt[n][:]
-            if kind == "half":
-                w32 = w32.rearrange("p j k -> p (j k)")
-            w32 = w32.bitcast(F32)
+            kind, ci, part = units[k]
+            w32 = wt[ci][:].bitcast(F32)
             if kind == "block":
                 grouped[k] = gpool.tile([P, K], BF16, name="grouped", tag="grouped", align_bytes=64)
-                colmaps = [row_block_cols(gp) for gp in range(2)]
+                banks = [
+                    (gp, [[part * 1024 + (2 * gp + s) * 2 * P + u for s in range(2)] for u in range(2)], False)
+                    for gp in range(2)
+                ]
             else:
                 grouped[k] = gpool.tile([P, 2 * K], BF16, name="grouped", tag="grouped", align_bytes=64)
-                rowlen = 1024 if kind == "whole" else 512
-                first = 2 * part if kind == "whole" else 0
-                colmaps = [
-                    [[(2 * jp + s) * rowlen + (first + gg) * 2 * P + u for s in range(2)] for u in range(2)]
-                    for gg in range(2)
-                    for jp in range(2)
-                ]
-            for slot in range(len(colmaps)):
-                if is_reordered(k) and slot >= 2:
-                    jp = slot - 2
-                    flat = ordered[k][:].rearrange("q j u p -> q (j u p)")
-                    cols = [[((2 * jp + s) * 2 + u) * P for s in range(2)] for u in range(2)]
-                    bank = transpose_bank(flat, cols, 1)
+                banks = []
+                for jp in range(2):
+                    for gg in range(2):
+                        if is_reordered(k) and gg == 1:
+                            cols = [[((2 * jp + s) * 2 + u) * P for s in range(2)] for u in range(2)]
+                        else:
+                            cols = [[word_of(ci, 2 * jp + s, 2 * part + gg) + u for s in range(2)] for u in range(2)]
+                        banks.append((2 * gg + jp, cols, is_reordered(k) and gg == 1))
+                if ci not in PIECES:
+                    banks = [b for b in banks if b[0] < 2] + [b for b in banks if b[0] >= 2]
+            for i, (slot, cols, is_ordered) in enumerate(banks):
+                if is_ordered:
+                    bank = transpose_bank(ordered[k][:].rearrange("q j u p -> q (j u p)"), cols, 1)
                 else:
-                    bank = transpose_bank(w32, colmaps[slot])
-                if engines is None and k >= NMAIN - 1:
+                    bank = transpose_bank(w32, cols)
+                if engines is not None:
+                    eng = engines[i]
+                elif k >= NMAIN - 1:
                     eng = "S"
-                elif engines is None:
-                    eng = "V" if banks_done["n"] % 8 in (V_BANKS_EARLY if k < EARLY_UNITS else V_BANKS) else "S"
                 else:
-                    eng = engines[slot]
+                    eng = "V" if banks_done["n"] % 16 in (V_BANKS_EARLY if k < EARLY_UNITS else V_BANKS) else "S"
                 banks_done["n"] = banks_done["n"] + 1
-                copy_bank(eng, grouped[k], slot, bank)
+                if eng == "V" and k >= EARLY_UNITS:
+                    vector_copies.append((grouped[k], slot, bank))
+                else:
+                    copy_bank(eng, grouped[k], slot, bank)
 
         def unit_q(k):
-            width = NCOL if units[k][1] == "block" else 2 * NCOL
+            width = NCOL if units[k][0] == "block" else 2 * NCOL
             codes[k] = cpool.tile([P, width], U32, name="codes", tag="codes", align_bytes=64)
             scales[k] = cpool.tile([P, width], U8, name="scales", tag="scales", align_bytes=64)
             nc.vector.quantize_mx(
@@ -314,9 +315,9 @@ def tile_naivelstm_pb_kernel(
         def chunk_mx(ci):
             wsel, a = CHUNKS[ci]
             gate, opnd = divmod(wsel, 2)
-            alone = (wsel, a) == (2, 3)
+            alone = ci == LAST - 1
             if opnd == 0:
-                bank = ACC_BANK[(gate, a)]
+                bank = a % 2
                 acc[gate] = accp.tile([P, NCOL], F32, name="acc%d" % bank, tag="acc%d" % bank)
             for g in range(4):
                 mx(
@@ -360,11 +361,11 @@ def tile_naivelstm_pb_kernel(
                 in1=igT[:, a, :, :].rearrange("p j q -> p q j"),
                 op=ALU.add,
             )
+            if a == 3:
+                store(out_1, cn_all[:])
 
         def ep_tanh(a):
             cols = slice(a * NCOL, (a + 1) * NCOL)
-            if a == 3:
-                store(out_1, cn_all[:])
             th[a] = ep.tile([P, NCOL], F32, name="th", tag="th")
             nc.scalar.activation(out=th[a][:], in_=cn_all[:, cols], func=ACT.Tanh)
 
@@ -380,8 +381,8 @@ def tile_naivelstm_pb_kernel(
                 defer(slot + 1, lambda: ep_z(a, 0))
                 defer(slot + 2, ep_sig)
                 defer(slot + 3, lambda: ep_cnext(a))
-                defer(slot + 4, lambda: ep_tanh(a))
             if wsel == 3:
+                defer(slot + 1, lambda: ep_tanh(a))
                 defer(slot + 1, lambda: ep_z(a, 1))
                 defer(slot + 2, ep_sig)
                 defer(slot + 3, lambda: ep_hnext(a))
@@ -408,26 +409,26 @@ def tile_naivelstm_pb_kernel(
             if j == 3:
                 store(out_0[:, cols], hn_all[:, cols])
 
+        prepare_h()
         for k in range(NMAIN):
             if is_reordered(k + 1):
                 unit_r(k + 1)
             unit_t(k)
             loads_after(k)
-            if k >= 1:
-                unit_q(k - 1)
-            if k == X_AT:
-                prepare_x()
-            if k == H_AT:
-                prepare_h()
             if k == X_AT + 1:
                 quantise_act(0)
-            if k == H_AT + 1:
+            if k >= 1:
+                unit_q(k - 1)
+            late_vector_copies()
+            if k == X_AT:
+                prepare_x()
+            if k == 0:
                 quantise_act(1)
             if k == IG_AT:
                 prepare_ig()
             for n in range(8):
                 if BIAS_AT[n] == k:
-                    spread_bias(n % 2, n // 2)
+                    spread_bias(n // 4, n % 4)
             if k % 2 == 1 and k >= 3:
                 chunk_mx((k - 3) // 2)
                 schedule_epilogue(k, (k - 3) // 2)
@@ -446,6 +447,7 @@ def tile_naivelstm_pb_kernel(
         unit_q(NMAIN + 1)
         late(NMAIN + 2)
         ep_z(3, 1)
+        ep_tanh(3)
         state["zpart"] = state["z"]
         unit_t(NMAIN + 3, "SS")
         unit_q(NMAIN + 2)

@@ -312,18 +312,17 @@ def tile_naivelstm_pb_kernel(
                 stop=stop,
             )
 
-        def chunk_mx(ci):
+        def unit_mx(k):
+            kind, ci, part = units[k]
             wsel, a = CHUNKS[ci]
             gate, opnd = divmod(wsel, 2)
-            alone = ci == LAST - 1
-            if opnd == 0:
-                bank = a % 2
-                acc[gate] = accp.tile([P, NCOL], F32, name="acc%d" % bank, tag="acc%d" % bank)
-            for g in range(4):
-                mx(
-                    acc[gate][:], opnd, g, 2 * ci + g // 2, slice((g % 2) * NCOL, (g % 2 + 1) * NCOL),
-                    opnd == 0 and g == 0, (opnd == 1 or alone) and g == 3,
-                )
+            first, last = 2 * part, 2 * part + 1
+            if opnd == 0 and part == 0:
+                acc[gate, a] = accp.tile([P, NCOL], F32, name="acc%d" % (a % 2), tag="acc%d" % (a % 2))
+            closes = part == 1 and (opnd == 1 or ci == LAST - 1)
+            for g in (first, last):
+                cols = slice((g - first) * NCOL, (g - first + 1) * NCOL)
+                mx(acc[gate, a][:], opnd, g, k, cols, opnd == 0 and g == 0, closes and g == last)
 
         def block_mx(j):
             if j == 0:
@@ -340,7 +339,7 @@ def tile_naivelstm_pb_kernel(
             z = ep.tile([P, NCOL], F32, name="z", tag="z")
             nc.vector.tensor_tensor(
                 out=natural(z[:]),
-                in0=acc[gate][:].rearrange("p (j q) -> p q j", j=4),
+                in0=acc[gate, a][:].rearrange("p (j q) -> p q j", j=4),
                 in1=natural(bias[:, gate * HID + a * NCOL : gate * HID + (a + 1) * NCOL]),
                 op=ALU.add,
             )
@@ -429,19 +428,22 @@ def tile_naivelstm_pb_kernel(
             for n in range(8):
                 if BIAS_AT[n] == k:
                     spread_bias(n // 4, n % 4)
+            if k >= 3:
+                for n in range(2 if k == 3 else 1):
+                    unit_mx(k - 2 if k > 3 else n)
             if k % 2 == 1 and k >= 3:
-                chunk_mx((k - 3) // 2)
                 schedule_epilogue(k, (k - 3) // 2)
             late(k)
 
         unit_t(NMAIN, "SS")
         loads_after(NMAIN)
         unit_q(NMAIN - 1)
+        unit_mx(NMAIN - 2)
         late(NMAIN)
         unit_t(NMAIN + 1, "SS")
         loads_after(NMAIN + 1)
         unit_q(NMAIN)
-        chunk_mx(LAST - 1)
+        unit_mx(NMAIN - 1)
         late(NMAIN + 1)
         unit_t(NMAIN + 2, "SS")
         unit_q(NMAIN + 1)

@@ -17,22 +17,27 @@ K = 2048
 HID = 2048
 NCOL = 512
 WBUFS = 6
-V_BANKS = (2,)
-V_BANKS_EARLY = (1, 5, 9, 13)
 EARLY_UNITS = 6
-REORDER_FROM = 6
+REORDER_FROM = 5
 PIECES = {
     0: ((0, 0, 2), (0, 2, 4), (1, 0, 2), (1, 2, 4)),
     1: ((0, 0, 4), (1, 0, 4)),
 }
 BIAS_AT = (2, 2, 2, 2, 3, 3, 4, 4)
 X_AT = 2
-IG_AT = 7
+LOAD_IG_BEHIND = 6
 
 FLOPS = 2 * 4 * 2048 * 2048 * 128
 
-CHUNKS = [(2 * gate + opnd, a) for gate in range(2) for a in range(4) for opnd in range(2)]
+BLOCKS = ((1, 0), (1, 1), (0, 0), (0, 1), (0, 2), (0, 3), (1, 2), (1, 3))
+CHUNKS = [(2 * gate + opnd, a) for gate, a in BLOCKS for opnd in range(2)]
 LAST = len(CHUNKS) - 1
+
+
+def vector_bank(k):
+    if k < EARLY_UNITS:
+        return 1
+    return 3 if k % 2 == 0 else None
 
 
 def tile_naivelstm_pb_kernel(
@@ -123,20 +128,24 @@ def tile_naivelstm_pb_kernel(
         load_piece(1, 1)
         load(2)
         load(3)
-        nc.sync.dma_start(out=ig_sb[:], in_=ig.rearrange("(a q j) b -> q a (j b)", a=4, q=P, j=4))
-        nc.sync.dma_start(out=c_sb[:], in_=c)
         progress = {"loaded": 4, "freed": 0}
+
+        def load_next():
+            n = progress["loaded"]
+            load(n)
+            progress["loaded"] = n + 1
+            if n == LOAD_IG_BEHIND:
+                nc.sync.dma_start(out=ig_sb[:], in_=ig.rearrange("(a q j) b -> q a (j b)", a=4, q=P, j=4))
+                nc.sync.dma_start(out=c_sb[:], in_=c)
 
         def loads_after(k):
             if k % 2 == 1 and k < NMAIN:
                 progress["freed"] = progress["freed"] + 1
             while progress["loaded"] <= LAST and progress["loaded"] - progress["freed"] < WBUFS:
-                load(progress["loaded"])
-                progress["loaded"] = progress["loaded"] + 1
+                load_next()
 
         while progress["loaded"] < WBUFS:
-            load(progress["loaded"])
-            progress["loaded"] = progress["loaded"] + 1
+            load_next()
 
         def transpose_bank(src32, cols, step=2):
             bank = tp.tile([P, 2, 2, P], F32, name="xt", tag="xt")
@@ -186,19 +195,12 @@ def tile_naivelstm_pb_kernel(
                 out=act_codes[opnd][:].bitcast(FP8X4), scales=act_scales[opnd][:], in_=act_grouped[opnd][:]
             )
 
-        igT = const.tile([P, 4, 4, P], BF16, name="igT")
+        igbank = {}
 
-        def prepare_ig():
-            for half in range(2):
-                ibank = tp.tile([P, 2, 4, P], BF16, name="ibank", tag="xt")
-                for a2 in range(2):
-                    for j in range(4):
-                        nc.tensor.transpose(
-                            ibank[:, a2, j, :],
-                            ig_sb[:, 2 * half + a2, j * P : (j + 1) * P],
-                            identb[:],
-                        )
-                nc.scalar.copy(out=igT[:, 2 * half : 2 * half + 2, :, :], in_=ibank[:])
+        def transpose_ig(a):
+            igbank[a] = tp.tile([P, 4, P], BF16, name="igbank", tag="xt")
+            for j in range(4):
+                nc.tensor.transpose(igbank[a][:, j, :], ig_sb[:, a, j * P : (j + 1) * P], identb[:])
 
         bias = const.tile([P, 2 * HID], F32, name="bias")
 
@@ -221,7 +223,6 @@ def tile_naivelstm_pb_kernel(
         th = {}
         blk = {}
         deferred = {}
-        banks_done = {"n": 0}
 
         def defer(slot, fn):
             deferred[slot] = deferred.get(slot, []) + [fn]
@@ -233,7 +234,7 @@ def tile_naivelstm_pb_kernel(
         ordered = {}
 
         def is_reordered(k):
-            return k >= REORDER_FROM and k < NMAIN
+            return k >= REORDER_FROM and k < NMAIN and (k < 10 or k % 4 != 2)
 
         def unit_r(k):
             kind, ci, part = units[k]
@@ -286,8 +287,7 @@ def tile_naivelstm_pb_kernel(
                 elif k >= NMAIN - 1:
                     eng = "S"
                 else:
-                    eng = "V" if banks_done["n"] % 16 in (V_BANKS_EARLY if k < EARLY_UNITS else V_BANKS) else "S"
-                banks_done["n"] = banks_done["n"] + 1
+                    eng = "V" if i == vector_bank(k) else "S"
                 if eng == "V" and k >= EARLY_UNITS:
                     vector_copies.append((grouped[k], slot, bank))
                 else:
@@ -350,14 +350,27 @@ def tile_naivelstm_pb_kernel(
             nc.scalar.activation(out=s[:], in_=state["z"][:], func=ACT.Sigmoid)
             state["s"] = s
 
-        def ep_cnext(a):
+        def ep_early_sig(a):
+            nc.scalar.activation(out=hn_all[:, a * NCOL : (a + 1) * NCOL], in_=state["z"][:], func=ACT.Sigmoid)
+
+        def ep_early_hnext(a):
             cols = slice(a * NCOL, (a + 1) * NCOL)
+            nc.vector.tensor_tensor(out=hn_all[:, cols], in0=hn_all[:, cols], in1=th[a][:], op=ALU.mult)
+
+        def ep_fc(a):
             t = ep.tile([P, NCOL], F32, name="fc", tag="fc")
-            nc.vector.tensor_tensor(out=t[:], in0=state["s"][:], in1=c_sb[:, cols], op=ALU.mult)
+            nc.vector.tensor_tensor(
+                out=t[:], in0=state["s"][:], in1=c_sb[:, a * NCOL : (a + 1) * NCOL], op=ALU.mult
+            )
+            state["fc"] = t
+
+        def ep_cnext(a):
+            transpose_ig(a)
+            cols = slice(a * NCOL, (a + 1) * NCOL)
             nc.vector.tensor_tensor(
                 out=natural(cn_all[:, cols]),
-                in0=natural(t[:]),
-                in1=igT[:, a, :, :].rearrange("p j q -> p q j"),
+                in0=natural(state["fc"][:]),
+                in1=igbank[a][:].rearrange("p j q -> p q j"),
                 op=ALU.add,
             )
             if a == 3:
@@ -379,8 +392,15 @@ def tile_naivelstm_pb_kernel(
             if wsel == 1:
                 defer(slot + 1, lambda: ep_z(a, 0))
                 defer(slot + 2, ep_sig)
-                defer(slot + 3, lambda: ep_cnext(a))
-            if wsel == 3:
+                defer(slot + 3, lambda: ep_fc(a))
+                defer(slot + 4, lambda: ep_cnext(a))
+                if a < 2:
+                    defer(slot + 5, lambda: ep_tanh(a))
+                    defer(slot + 6, lambda: ep_early_hnext(a))
+            if wsel == 3 and a < 2:
+                defer(slot + 1, lambda: ep_z(a, 1))
+                defer(slot + 2, lambda: ep_early_sig(a))
+            if wsel == 3 and a >= 2:
                 defer(slot + 1, lambda: ep_tanh(a))
                 defer(slot + 1, lambda: ep_z(a, 1))
                 defer(slot + 2, ep_sig)
@@ -423,14 +443,12 @@ def tile_naivelstm_pb_kernel(
                 prepare_x()
             if k == 0:
                 quantise_act(1)
-            if k == IG_AT:
-                prepare_ig()
             for n in range(8):
                 if BIAS_AT[n] == k:
-                    spread_bias(n // 4, n % 4)
-            if k >= 3:
-                for n in range(2 if k == 3 else 1):
-                    unit_mx(k - 2 if k > 3 else n)
+                    spread_bias(*BLOCKS[n])
+            if k % 2 == 1 and k >= 3:
+                unit_mx(k - 3)
+                unit_mx(k - 2)
             if k % 2 == 1 and k >= 3:
                 schedule_epilogue(k, (k - 3) // 2)
             late(k)
@@ -438,11 +456,11 @@ def tile_naivelstm_pb_kernel(
         unit_t(NMAIN, "SS")
         loads_after(NMAIN)
         unit_q(NMAIN - 1)
-        unit_mx(NMAIN - 2)
         late(NMAIN)
         unit_t(NMAIN + 1, "SS")
         loads_after(NMAIN + 1)
         unit_q(NMAIN)
+        unit_mx(NMAIN - 2)
         unit_mx(NMAIN - 1)
         late(NMAIN + 1)
         unit_t(NMAIN + 2, "SS")

@@ -234,7 +234,7 @@ def tile_naivelstm_pb_kernel(
         ordered = {}
 
         def is_reordered(k):
-            return k >= REORDER_FROM and k < NMAIN and (k < 10 or k % 4 != 2)
+            return k >= REORDER_FROM and k < NMAIN and (k < 18 or k % 4 != 2)
 
         def unit_r(k):
             kind, ci, part = units[k]
@@ -288,7 +288,7 @@ def tile_naivelstm_pb_kernel(
                     eng = "S"
                 else:
                     eng = "V" if i == vector_bank(k) else "S"
-                if eng == "V" and k >= EARLY_UNITS:
+                if eng == "V" and k >= EARLY_UNITS and engines is None:
                     vector_copies.append((grouped[k], slot, bank))
                 else:
                     copy_bank(eng, grouped[k], slot, bank)
@@ -469,19 +469,15 @@ def tile_naivelstm_pb_kernel(
         ep_z(3, 1)
         ep_tanh(3)
         state["zpart"] = state["z"]
-        unit_t(NMAIN + 3, "SS")
+        unit_t(NMAIN + 3, "VS")
         unit_q(NMAIN + 2)
         late(NMAIN + 3)
         for j in range(3):
             block_mx(j)
         unit_q(NMAIN + 3)
         block_mx(3)
-        for j in range(3):
+        for j in range(4):
             last_z(j)
             last_sig(j)
-        last_h(0)
-        last_h(1)
-        last_z(3)
-        last_sig(3)
-        last_h(2)
-        last_h(3)
+        for j in range(4):
+            last_h(j)

@@ -37,7 +37,7 @@ LAST = len(CHUNKS) - 1
 def vector_bank(k):
     if k < EARLY_UNITS:
         return 1
-    return 3 if k % 2 == 0 else None
+    return 3 if k % 3 == 0 else None
 
 
 def tile_naivelstm_pb_kernel(
@@ -234,7 +234,7 @@ def tile_naivelstm_pb_kernel(
         ordered = {}
 
         def is_reordered(k):
-            return k >= REORDER_FROM and k < NMAIN and (k < 18 or k % 4 != 2)
+            return k >= REORDER_FROM and k < NMAIN
 
         def unit_r(k):
             kind, ci, part = units[k]

from contextlib import ExitStack

import concourse.mybir as mybir
from concourse.masks import make_identity

F32 = mybir.dt.float32
BF16 = mybir.dt.bfloat16
U32 = mybir.dt.uint32
U8 = mybir.dt.uint8
I32 = mybir.dt.int32
FP8X4 = mybir.dt.float8_e4m3fn_x4
ACT = mybir.ActivationFunctionType
ALU = mybir.AluOpType

P = 128
K = 2048
HID = 2048
NCOL = 512
WBUFS = 6
EARLY_UNITS = 6
REORDER_FROM = 5
PIECES = {
    0: ((0, 0, 2), (0, 2, 4), (1, 0, 2), (1, 2, 4)),
    1: ((0, 0, 4), (1, 0, 4)),
}
BIAS_AT = (2, 2, 2, 2, 3, 3, 4, 4)
X_AT = 2
LOAD_IG_BEHIND = 6

FLOPS = 2 * 4 * 2048 * 2048 * 128

BLOCKS = ((1, 0), (1, 1), (0, 0), (0, 1), (0, 2), (0, 3), (1, 2), (1, 3))
CHUNKS = [(2 * gate + opnd, a) for gate, a in BLOCKS for opnd in range(2)]
LAST = len(CHUNKS) - 1


def vector_bank(k):
    if k < EARLY_UNITS:
        return 1
    return 3 if k % 3 == 0 else None


def tile_naivelstm_pb_kernel(
    tc, x, h, c, ig, w_if, w_io, w_hf, w_ho, b_if, b_hf, b_io, b_ho, out_0, out_1
):
    nc = tc.nc
    with ExitStack() as ctx:
        ctx.enter_context(tc.manual_schedule())
        const = ctx.enter_context(tc.tile_pool(name="const", bufs=1))
        wpool = ctx.enter_context(tc.tile_pool(name="wpool", bufs=WBUFS))
        gpool = ctx.enter_context(tc.tile_pool(name="gpool", bufs=3))
        rpool = ctx.enter_context(tc.tile_pool(name="rpool", bufs=3))
        cpool = ctx.enter_context(tc.tile_pool(name="cpool", bufs=5))
        ep = ctx.enter_context(tc.tile_pool(name="ep", bufs=2))
        accp = ctx.enter_context(tc.psum_pool(name="accp", bufs=1))
        tp = ctx.enter_context(tc.psum_pool(name="tp", bufs=6))

        weights = (w_if, w_hf, w_io, w_ho)

        ident32 = const.tile([P, P], F32, name="ident32")
        identb = const.tile([P, P], BF16, name="identb")
        brows = const.tile([P, NCOL], BF16, name="brows")
        nc.vector.memset(brows[:].bitcast(I32), 0)
        for first_row, b in ((0, b_if), (1, b_hf), (2, b_io), (3, b_ho)):
            nc.scalar.dma_start(
                out=brows[first_row : 16 : 4, :], in_=b.rearrange("(a n) o -> a (n o)", a=4)
            )
        make_identity(nc, identb[:])
        make_identity(nc, ident32[:])
        pairsel = const.tile([P, 8], BF16, name="pairsel")
        nc.vector.tensor_tensor(out=pairsel[:], in0=identb[:, 0:16:2], in1=identb[:, 1:16:2], op=ALU.add)
        warm = const.tile([P, 2], F32, name="warm")
        nc.vector.memset(warm[:], 0.0)
        nc.scalar.activation(out=warm[:, 1:2], in_=warm[:, 0:1], func=ACT.Sigmoid)

        units = [("wide", ci, gp) for ci in range(LAST) for gp in range(2)]
        NMAIN = len(units)
        units = units + [("block", LAST, j) for j in range(4)]

        wt = {}
        pieces_of = {}
        stores = {"open": False, "pending": []}

        def weight_tile(ci):
            wt[ci] = wpool.tile([P, 4 * K], BF16, name="wt", tag="wt")
            wsel, a = CHUNKS[ci]
            return wt[ci][:], weights[wsel][a * NCOL : (a + 1) * NCOL, :]

        def load_piece(ci, i):
            half, j0, j1 = PIECES[ci][i]
            if i == 0:
                pieces_of[ci] = weight_tile(ci)
            t, rows = pieces_of[ci]
            nc.sync.dma_start(
                out=t.rearrange("q (h j k) -> q h j k", h=2, j=4)[:, half, j0:j1, :],
                in_=rows.rearrange("(q j) (h k) -> q h j k", j=4, h=2)[:, half, j0:j1, :],
            )

        def load(ci):
            if ci in PIECES:
                for i in range(len(PIECES[ci])):
                    load_piece(ci, i)
                return
            t, rows = weight_tile(ci)
            if ci < LAST:
                nc.sync.dma_start(out=t, in_=rows.rearrange("(q j) k -> q (j k)", j=4))
            else:
                for j in range(4):
                    nc.sync.dma_start(out=t[:, j * K : (j + 1) * K], in_=rows[j * P : (j + 1) * P, :])
                stores["open"] = True
                for dst, src in stores["pending"]:
                    nc.sync.dma_start(out=dst, in_=src)

        def store(dst, src):
            if stores["open"]:
                nc.sync.dma_start(out=dst, in_=src)
            else:
                stores["pending"].append((dst, src))

        h_sb = const.tile([P, K], BF16, name="h_sb")
        xraw = const.tile([P, 4, 4, P], BF16, name="xraw")
        ig_sb = const.tile([P, 4, 4 * P], BF16, name="ig_sb")
        c_sb = const.tile([P, HID], BF16, name="c_sb")
        nc.sync.dma_start(out=h_sb[:], in_=h)
        load(0)
        load_piece(1, 0)
        nc.sync.dma_start(out=xraw[:], in_=x.rearrange("(g p t) b -> p g t b", g=4, p=P, t=4))
        load_piece(1, 1)
        load(2)
        load(3)
        progress = {"loaded": 4, "freed": 0}

        def load_next():
            n = progress["loaded"]
            load(n)
            progress["loaded"] = n + 1
            if n == LOAD_IG_BEHIND:
                nc.sync.dma_start(out=ig_sb[:], in_=ig.rearrange("(a q j) b -> q a (j b)", a=4, q=P, j=4))
                nc.sync.dma_start(out=c_sb[:], in_=c)

        def loads_after(k):
            if k % 2 == 1 and k < NMAIN:
                progress["freed"] = progress["freed"] + 1
            while progress["loaded"] <= LAST and progress["loaded"] - progress["freed"] < WBUFS:
                load_next()

        while progress["loaded"] < WBUFS:
            load_next()

        def transpose_bank(src32, cols, step=2):
            bank = tp.tile([P, 2, 2, P], F32, name="xt", tag="xt")
            for u in range(2):
                for s in range(2):
                    col = cols[u][s]
                    nc.tensor.transpose(bank[:, u, s, :], src32[:, col : col + step * (P - 1) + 1 : step], ident32[:])
            return bank

        def copy_bank(eng, grouped, slot, bank):
            dst = grouped[:].bitcast(F32).rearrange("p (n u) -> p n u", u=2)
            dst = dst[:, slot * 256 : (slot + 1) * 256, :]
            src = bank[:].rearrange("p u s q -> p (s q) u")
            if eng == "S":
                nc.scalar.copy(out=dst, in_=src)
            else:
                nc.vector.tensor_copy(out=dst, in_=src)

        def row_block_cols(gp):
            return [[(2 * gp + s) * 2 * P + u for s in range(2)] for u in range(2)]

        act_codes = []
        act_scales = []
        for nm in ("x", "h"):
            act_codes.append(const.tile([P, 512], U32, name="codes_" + nm, align_bytes=64))
            act_scales.append(const.tile([P, 512], U8, name="scales_" + nm, align_bytes=64))
        act_grouped = {}

        def prepare_x():
            xg = gpool.tile([P, K], BF16, name="grouped", tag="grouped", align_bytes=64)
            nc.vector.tensor_copy(
                out=xg[:].rearrange("p (g b t) -> p g b t", g=4, b=P, t=4),
                in_=xraw[:].rearrange("p g t b -> p g b t"),
            )
            act_grouped[0] = xg

        def prepare_h():
            h32 = h_sb[:].bitcast(F32)
            hg = gpool.tile([P, K], BF16, name="grouped", tag="grouped", align_bytes=64)
            hbanks = [transpose_bank(h32, row_block_cols(gp)) for gp in range(2)]
            for gp in range(2):
                copy_bank("V", hg, gp, hbanks[gp])
            act_grouped[1] = hg

        def quantise_act(opnd):
            nc.vector.quantize_mx(
                out=act_codes[opnd][:].bitcast(FP8X4), scales=act_scales[opnd][:], in_=act_grouped[opnd][:]
            )

        igbank = {}

        def transpose_ig(a):
            igbank[a] = tp.tile([P, 4, P], BF16, name="igbank", tag="xt")
            for j in range(4):
                nc.tensor.transpose(igbank[a][:, j, :], ig_sb[:, a, j * P : (j + 1) * P], identb[:])

        bias = const.tile([P, 2 * HID], F32, name="bias")

        def spread_bias(gate, a):
            cols = slice(gate * HID + a * NCOL, gate * HID + (a + 1) * NCOL)
            bbank = tp.tile([P, NCOL], F32, name="bbank", tag="xt")
            i = 2 * a + gate
            nc.tensor.matmul(
                out=bbank[:], lhsT=pairsel[:, i : i + 1].to_broadcast([P, P]), rhs=brows[:], start=True, stop=True
            )
            nc.scalar.copy(out=bias[:, cols], in_=bbank[:])

        cn_all = const.tile([P, HID], F32, name="cn_all")
        hn_all = const.tile([P, HID], F32, name="hn_all")
        grouped = {}
        codes = {}
        scales = {}
        acc = {}
        state = {}
        th = {}
        blk = {}
        deferred = {}

        def defer(slot, fn):
            deferred[slot] = deferred.get(slot, []) + [fn]

        def late(slot):
            for fn in deferred.get(slot, []):
                fn()

        ordered = {}

        def is_reordered(k):
            return k >= REORDER_FROM and k < NMAIN

        def unit_r(k):
            kind, ci, part = units[k]
            g = 2 * part + 1
            t = rpool.tile([P, 4, 2, P], F32, name="ordered", tag="ordered")
            src = wt[ci][:].bitcast(F32).rearrange("q (j g p u) -> q g j u p", j=4, g=4, u=2)
            nc.vector.tensor_copy(out=t[:], in_=src[:, g, :, :, :])
            ordered[k] = t

        def word_of(ci, j, g):
            if ci in PIECES:
                return (g // 2) * 2048 + j * 512 + (g % 2) * 256
            return j * 1024 + g * 256

        vector_copies = []

        def late_vector_copies():
            for dst, slot, bank in vector_copies:
                copy_bank("V", dst, slot, bank)
            vector_copies.clear()

        def unit_t(k, engines=None):
            kind, ci, part = units[k]
            w32 = wt[ci][:].bitcast(F32)
            if kind == "block":
                grouped[k] = gpool.tile([P, K], BF16, name="grouped", tag="grouped", align_bytes=64)
                banks = [
                    (gp, [[part * 1024 + (2 * gp + s) * 2 * P + u for s in range(2)] for u in range(2)], False)
                    for gp in range(2)
                ]
            else:
                grouped[k] = gpool.tile([P, 2 * K], BF16, name="grouped", tag="grouped", align_bytes=64)
                banks = []
                for jp in range(2):
                    for gg in range(2):
                        if is_reordered(k) and gg == 1:
                            cols = [[((2 * jp + s) * 2 + u) * P for s in range(2)] for u in range(2)]
                        else:
                            cols = [[word_of(ci, 2 * jp + s, 2 * part + gg) + u for s in range(2)] for u in range(2)]
                        banks.append((2 * gg + jp, cols, is_reordered(k) and gg == 1))
                if ci not in PIECES:
                    banks = [b for b in banks if b[0] < 2] + [b for b in banks if b[0] >= 2]
            for i, (slot, cols, is_ordered) in enumerate(banks):
                if is_ordered:
                    bank = transpose_bank(ordered[k][:].rearrange("q j u p -> q (j u p)"), cols, 1)
                else:
                    bank = transpose_bank(w32, cols)
                if engines is not None:
                    eng = engines[i]
                elif k >= NMAIN - 1:
                    eng = "S"
                else:
                    eng = "V" if i == vector_bank(k) else "S"
                if eng == "V" and k >= EARLY_UNITS and engines is None:
                    vector_copies.append((grouped[k], slot, bank))
                else:
                    copy_bank(eng, grouped[k], slot, bank)

        def unit_q(k):
            width = NCOL if units[k][0] == "block" else 2 * NCOL
            codes[k] = cpool.tile([P, width], U32, name="codes", tag="codes", align_bytes=64)
            scales[k] = cpool.tile([P, width], U8, name="scales", tag="scales", align_bytes=64)
            nc.vector.quantize_mx(
                out=codes[k][:].bitcast(FP8X4), scales=scales[k][:], in_=grouped[k][:]
            )

        def mx(out, opnd, g, k, cols, start, stop):
            nc.tensor.matmul_mx(
                out=out,
                lhsT=act_codes[opnd][:, g * P : (g + 1) * P].bitcast(FP8X4),
                lhsT_scale=act_scales[opnd][:, g * P : (g + 1) * P],
                rhs=codes[k][:, cols].bitcast(FP8X4),
                rhs_scale=scales[k][:, cols],
                start=start,
                stop=stop,
            )

        def unit_mx(k):
            kind, ci, part = units[k]
            wsel, a = CHUNKS[ci]
            gate, opnd = divmod(wsel, 2)
            first, last = 2 * part, 2 * part + 1
            if opnd == 0 and part == 0:
                acc[gate, a] = accp.tile([P, NCOL], F32, name="acc%d" % (a % 2), tag="acc%d" % (a % 2))
            closes = part == 1 and (opnd == 1 or ci == LAST - 1)
            for g in (first, last):
                cols = slice((g - first) * NCOL, (g - first + 1) * NCOL)
                mx(acc[gate, a][:], opnd, g, k, cols, opnd == 0 and g == 0, closes and g == last)

        def block_mx(j):
            if j == 0:
                blk[j] = accp.tile([P, P], F32, name="acc0", tag="acc0")
            else:
                blk[j] = tp.tile([P, P], F32, name="blk", tag="xt")
            for g in range(4):
                mx(blk[j][:], 1, g, NMAIN + j, slice(g * P, (g + 1) * P), g == 0, g == 3)

        def natural(ap):
            return ap.rearrange("p (q j) -> p q j", j=4)

        def ep_z(a, gate):
            z = ep.tile([P, NCOL], F32, name="z", tag="z")
            nc.vector.tensor_tensor(
                out=natural(z[:]),
                in0=acc[gate, a][:].rearrange("p (j q) -> p q j", j=4),
                in1=natural(bias[:, gate * HID + a * NCOL : gate * HID + (a + 1) * NCOL]),
                op=ALU.add,
            )
            state["z"] = z

        def ep_sig():
            s = ep.tile([P, NCOL], F32, name="sg", tag="sg")
            nc.scalar.activation(out=s[:], in_=state["z"][:], func=ACT.Sigmoid)
            state["s"] = s

        def ep_early_sig(a):
            nc.scalar.activation(out=hn_all[:, a * NCOL : (a + 1) * NCOL], in_=state["z"][:], func=ACT.Sigmoid)

        def ep_early_hnext(a):
            cols = slice(a * NCOL, (a + 1) * NCOL)
            nc.vector.tensor_tensor(out=hn_all[:, cols], in0=hn_all[:, cols], in1=th[a][:], op=ALU.mult)

        def ep_fc(a):
            t = ep.tile([P, NCOL], F32, name="fc", tag="fc")
            nc.vector.tensor_tensor(
                out=t[:], in0=state["s"][:], in1=c_sb[:, a * NCOL : (a + 1) * NCOL], op=ALU.mult
            )
            state["fc"] = t

        def ep_cnext(a):
            transpose_ig(a)
            cols = slice(a * NCOL, (a + 1) * NCOL)
            nc.vector.tensor_tensor(
                out=natural(cn_all[:, cols]),
                in0=natural(state["fc"][:]),
                in1=igbank[a][:].rearrange("p j q -> p q j"),
                op=ALU.add,
            )
            if a == 3:
                store(out_1, cn_all[:])

        def ep_tanh(a):
            cols = slice(a * NCOL, (a + 1) * NCOL)
            th[a] = ep.tile([P, NCOL], F32, name="th", tag="th")
            nc.scalar.activation(out=th[a][:], in_=cn_all[:, cols], func=ACT.Tanh)

        def ep_hnext(a):
            cols = slice(a * NCOL, (a + 1) * NCOL)
            nc.vector.tensor_tensor(out=hn_all[:, cols], in0=state["s"][:], in1=th[a][:], op=ALU.mult)
            if a == 2:
                store(out_0[:, 0 : 3 * NCOL], hn_all[:, 0 : 3 * NCOL])

        def schedule_epilogue(slot, ci):
            wsel, a = CHUNKS[ci]
            if wsel == 1:
                defer(slot + 1, lambda: ep_z(a, 0))
                defer(slot + 2, ep_sig)
                defer(slot + 3, lambda: ep_fc(a))
                defer(slot + 4, lambda: ep_cnext(a))
                if a < 2:
                    defer(slot + 5, lambda: ep_tanh(a))
                    defer(slot + 6, lambda: ep_early_hnext(a))
            if wsel == 3 and a < 2:
                defer(slot + 1, lambda: ep_z(a, 1))
                defer(slot + 2, lambda: ep_early_sig(a))
            if wsel == 3 and a >= 2:
                defer(slot + 1, lambda: ep_tanh(a))
                defer(slot + 1, lambda: ep_z(a, 1))
                defer(slot + 2, ep_sig)
                defer(slot + 3, lambda: ep_hnext(a))

        def last_z(j):
            zl = ep.tile([P, P], F32, name="zl", tag="zl", bufs=4)
            nc.vector.tensor_tensor(
                out=zl[:], in0=blk[j][:], in1=state["zpart"][:, j * P : (j + 1) * P], op=ALU.add
            )
            state["zl%d" % j] = zl

        def last_sig(j):
            sl = ep.tile([P, P], F32, name="sl", tag="sl", bufs=4)
            nc.scalar.activation(out=sl[:], in_=state["zl%d" % j][:], func=ACT.Sigmoid)
            state["sl%d" % j] = sl

        def last_h(j):
            cols = slice(3 * NCOL + j * P, 3 * NCOL + (j + 1) * P)
            nc.vector.tensor_tensor(
                out=hn_all[:, cols], in0=state["sl%d" % j][:], in1=th[3][:, j * P : (j + 1) * P], op=ALU.mult
            )
            if j == 2:
                store(out_0[:, 3 * NCOL : 3 * NCOL + 3 * P], hn_all[:, 3 * NCOL : 3 * NCOL + 3 * P])
            if j == 3:
                store(out_0[:, cols], hn_all[:, cols])

        prepare_h()
        for k in range(NMAIN):
            if is_reordered(k + 1):
                unit_r(k + 1)
            unit_t(k)
            loads_after(k)
            if k == X_AT + 1:
                quantise_act(0)
            if k >= 1:
                unit_q(k - 1)
            late_vector_copies()
            if k == X_AT:
                prepare_x()
            if k == 0:
                quantise_act(1)
            for n in range(8):
                if BIAS_AT[n] == k:
                    spread_bias(*BLOCKS[n])
            if k % 2 == 1 and k >= 3:
                unit_mx(k - 3)
                unit_mx(k - 2)
            if k % 2 == 1 and k >= 3:
                schedule_epilogue(k, (k - 3) // 2)
            late(k)

        unit_t(NMAIN, "SS")
        loads_after(NMAIN)
        unit_q(NMAIN - 1)
        late(NMAIN)
        unit_t(NMAIN + 1, "SS")
        loads_after(NMAIN + 1)
        unit_q(NMAIN)
        unit_mx(NMAIN - 2)
        unit_mx(NMAIN - 1)
        late(NMAIN + 1)
        unit_t(NMAIN + 2, "SS")
        unit_q(NMAIN + 1)
        late(NMAIN + 2)
        ep_z(3, 1)
        ep_tanh(3)
        state["zpart"] = state["z"]
        unit_t(NMAIN + 3, "VS")
        unit_q(NMAIN + 2)
        late(NMAIN + 3)
        for j in range(3):
            block_mx(j)
        unit_q(NMAIN + 3)
        block_mx(3)
        for j in range(4):
            last_z(j)
            last_sig(j)
        for j in range(4):
            last_h(j)
